import numpy as np
import ml_dtypes


def mxq(x, axis, fmt="e4m3"):
    dtype, down = {"e4m3": (ml_dtypes.float8_e4m3fn, 7), "e5m2": (ml_dtypes.float8_e5m2, 14)}[fmt]
    v = np.moveaxis(np.asarray(x, np.float32).astype(ml_dtypes.bfloat16).astype(np.float64), axis, -1)
    blocks = v.reshape(v.shape[:-1] + (-1, 32))
    amax = np.abs(blocks).max(-1, keepdims=True)
    byte = np.maximum(np.where(amax > 0, np.frexp(amax)[1] - 1 + 127, 0) - down, 1)
    scale = np.exp2(byte - 127.0)
    codes = (blocks / scale).astype(np.float32).astype(dtype).astype(np.float64)
    return np.moveaxis((codes * scale).reshape(v.shape), -1, axis)


WIDE = False


def mx_kscale(k):
    if not WIDE:
        return np.ones(k)
    levels = np.array([10, -10, 5, -5, 0])
    a = np.random.permutation(np.resize(levels, k // 512 * 4)).reshape(k // 512, 4)
    idx = np.arange(k)
    return np.exp2(a[idx // 512, idx % 128 // 32])


BF16 = ml_dtypes.bfloat16


def bf(x):
    return np.asarray(x, np.float32).astype(BF16)


def f64(x):
    return np.asarray(x).astype(np.float64)


B, S, D_IN, D_OUT = 16, 256, 512, 512


def gelu_tanh(x):
    return 0.5 * x * (1.0 + np.tanh(x * 0.7978845608 * (1.0 + 0.044715 * x * x)))


def wn_weight(v, g):
    return v * (g / np.sqrt((v * v).sum(axis=1)))[:, None]


def setup_inputs():
    s = mx_kscale(D_IN)
    v1 = bf(np.random.standard_normal((D_OUT, D_IN)) * np.sqrt(2.0 / D_IN) / s[None, :])
    g1 = bf(np.sqrt((f64(v1) * f64(v1)).sum(axis=1)) * (1.0 + 0.1 * np.random.standard_normal(D_OUT)))
    return {"head": bf(np.random.standard_normal((B, S, D_IN)) * s),
            "tail": bf(np.random.standard_normal((B, S, D_IN)) * s),
            "v1": v1, "g1": g1, "b1": bf(0.3 * np.random.standard_normal(D_OUT))}


def reference(head, tail, v1, g1, b1):
    w1q = mxq(wn_weight(f64(v1), f64(g1)), 1, "e4m3")
    h = gelu_tanh((mxq(f64(head), 2, "e4m3") @ w1q.T) + f64(b1))
    t = gelu_tanh((mxq(f64(tail), 2, "e4m3") @ w1q.T) + f64(b1))
    attn = (mxq(h, 2, "e4m3") @ mxq(t, 2, "e4m3").transpose(0, 2, 1)) * (1.0 / np.sqrt(D_OUT))
    return attn, h, t

@@ -1,0 +1,293 @@
+import math
+from contextlib import ExitStack
+
+import concourse.bass as bass
+import concourse.mybir as mybir
+import concourse.tile as tile
+from concourse.masks import make_identity
+
+F32 = mybir.dt.float32
+BF16 = mybir.dt.bfloat16
+U32 = mybir.dt.uint32
+U8 = mybir.dt.uint8
+FP8X4 = mybir.dt.float8_e4m3fn_x4
+ACT = mybir.ActivationFunctionType
+ALU = mybir.AluOpType
+
+P = 128
+B, S, D = 16, 256, 512
+FLOPS = 2 * (2 * B * S) * D * D + 2 * B * S * S * D
+
+MANUAL = True
+LX = 4
+A_ENG = "v"
+
+
+def tile_mappedattention_pa_t_kernel(tc, head, tail, v1, g1, b1, out_0, out_1, out_2):
+    nc = tc.nc
+    inv_sqrt_d = 1.0 / math.sqrt(float(D))
+    streams = (head, tail)
+    h_outs = (out_1, out_2)
+
+    with ExitStack() as ctx:
+        const = ctx.enter_context(tc.tile_pool(name="const", bufs=1))
+        xin = ctx.enter_context(tc.tile_pool(name="xin", bufs=1))
+        xgp = ctx.enter_context(tc.tile_pool(name="xgp", bufs=3))
+        xcp = ctx.enter_context(tc.tile_pool(name="xcp", bufs=LX + 2))
+        htp = ctx.enter_context(tc.tile_pool(name="htp", bufs=3))
+        hgp = ctx.enter_context(tc.tile_pool(name="hgp", bufs=2))
+        hcp = ctx.enter_context(tc.tile_pool(name="hcp", bufs=3))
+        hop = ctx.enter_context(tc.tile_pool(name="hop", bufs=3))
+        atp = ctx.enter_context(tc.tile_pool(name="atp", bufs=3))
+        psum = ctx.enter_context(tc.psum_pool(name="psum", bufs=8))
+        if MANUAL:
+            ctx.enter_context(tc.manual_schedule())
+
+        def evac(eng, out, in_):
+            if eng == "v":
+                nc.vector.tensor_copy(out=out, in_=in_)
+            else:
+                nc.scalar.copy(out=out, in_=in_)
+
+        v_sb = const.tile([P, 4, D], BF16, name="v_sb")
+        nc.sync.dma_start(out=v_sb[:], in_=v1.rearrange("(p t) k -> p t k", t=4))
+        g_sb = const.tile([P, 4], BF16, name="g_sb")
+        b_sb = const.tile([P, 4], BF16, name="b_sb")
+        with nc.allow_non_contiguous_dma(reason="four bf16 values to a partition"):
+            nc.sync.dma_start(out=g_sb[:], in_=g1.rearrange("(p t) -> p t", t=4))
+            nc.sync.dma_start(out=b_sb[:], in_=b1.rearrange("(p t) -> p t", t=4))
+        x_sb = {}
+        for b in range(B):
+            for st in range(2):
+                xt = xin.tile([P, 2 * D], BF16, name="x%d_%d" % (st, b))
+                nc.sync.dma_start(out=xt[:], in_=streams[st][b].rearrange("(q j) k -> q (j k)", j=2))
+                x_sb[(st, b)] = xt
+
+        ident_f = const.tile([P, P], F32, name="ident_f")
+        make_identity(nc, ident_f[:])
+        ident_b = const.tile([P, P], BF16, name="ident_b")
+        make_identity(nc, ident_b[:])
+        dummy = const.tile([P, 1], F32, name="dummy")
+        nc.vector.memset(dummy[:], 1.0)
+        dummy2 = const.tile([P, 1], F32, name="dummy2")
+        nc.scalar.activation(out=dummy2[:], in_=dummy[:], func=ACT.Sqrt)
+
+        st_x = {}
+        st_xg = {}
+        st_xc = {}
+        st_z = {}
+        st_ht = {}
+        st_hg = {}
+        st_hc = {}
+        st_hp = {}
+        st_a = {}
+
+        def x_pe(i):
+            banks = []
+            for st in range(2):
+                xp = psum.tile([P, 2, 2, P], F32, name="xp", tag="ring")
+                xw = x_sb[(st, i)][:].bitcast(F32)
+                for j in range(2):
+                    for u in range(2):
+                        off = j * 256 + u * P
+                        nc.tensor.transpose(out=xp[:, j, u, :], in_=xw[:, off:off + P], identity=ident_f[:])
+                banks.append(xp)
+            st_x[i] = banks
+
+        def x_evac(i, engs):
+            xg = xgp.tile([P, 4 * P, 2], F32, name="xg", tag="xg", align_bytes=64)
+            for st in range(2):
+                evac(
+                    engs[st],
+                    xg[:, st * 256:(st + 1) * 256, :].rearrange("p (j q) u -> p j q u", j=2),
+                    st_x[i][st][:].rearrange("p j u q -> p j q u"),
+                )
+            st_xg[i] = xg
+
+        def x_quant(i):
+            xc = xcp.tile([P, 4 * P], U32, name="xc", tag="xc", align_bytes=64)
+            xs = xcp.tile([P, 4 * P], U8, name="xs", tag="xs", align_bytes=64)
+            nc.vector.quantize_mx(
+                out=xc[:].bitcast(FP8X4),
+                scales=xs[:],
+                in_=st_xg[i][:].rearrange("p c u -> p (c u)").bitcast(BF16),
+            )
+            st_xc[i] = (xc, xs)
+
+        def z_pe(i):
+            xc, xs = st_xc[i]
+            banks = []
+            for t in range(4):
+                zp = psum.tile([P, 4 * P], F32, name="zp", tag="ring")
+                nc.tensor.matmul_mx(
+                    out=zp[:],
+                    lhsT=wc[:, t * P:(t + 1) * P].bitcast(FP8X4),
+                    lhsT_scale=ws[:, t * P:(t + 1) * P],
+                    rhs=xc[:].bitcast(FP8X4),
+                    rhs_scale=xs[:],
+                    start=True,
+                    stop=True,
+                )
+                banks.append(zp)
+            st_z[i] = banks
+
+        def gelu(i):
+            ht = htp.tile([P, 4, 4 * P], F32, name="ht", tag="ht")
+            for t in range(4):
+                nc.scalar.activation(
+                    out=ht[:, t, :], in_=st_z[i][t][:], func=ACT.Gelu_apprx_tanh,
+                    bias=b_f[:, t:t + 1], scale=1.0,
+                )
+            st_ht[i] = ht
+
+        def regroup(i):
+            hg = hgp.tile([P, 4 * P, 4], BF16, name="hg", tag="hg", align_bytes=64)
+            nc.vector.tensor_copy(out=hg[:], in_=st_ht[i][:].rearrange("p t c -> p c t"))
+            st_hg[i] = hg
+
+        def h_quant(i):
+            hc = hcp.tile([P, 4 * P], U32, name="hc", tag="hc", align_bytes=64)
+            hs = hcp.tile([P, 4 * P], U8, name="hs", tag="hs", align_bytes=64)
+            nc.vector.quantize_mx(
+                out=hc[:].bitcast(FP8X4),
+                scales=hs[:],
+                in_=st_hg[i][:].rearrange("p c t -> p (c t)"),
+            )
+            st_hc[i] = (hc, hs)
+
+        def h_pe(i):
+            banks = []
+            for a in range(4):
+                hp = psum.tile([P, 4, P], F32, name="hp", tag="ring")
+                for t in range(4):
+                    nc.tensor.transpose(out=hp[:, t, :], in_=st_ht[i][:, t, a * P:(a + 1) * P], identity=ident_f[:])
+                banks.append(hp)
+            st_hp[i] = banks
+
+        def h_evac(i, engs):
+            ho = hop.tile([P, 4, D], F32, name="ho", tag="ho")
+            for a in range(4):
+                evac(
+                    engs[a],
+                    ho[:, a, :].rearrange("q (p t) -> q p t", t=4),
+                    st_hp[i][a][:].rearrange("q t p -> q p t"),
+                )
+                if a % 2 == 1:
+                    st = a // 2
+                    nc.sync.dma_start(
+                        out=h_outs[st][i].rearrange("(q j) o -> q j o", j=2),
+                        in_=ho[:, 2 * st:2 * st + 2, :],
+                    )
+
+        def a_pe(i):
+            hc, hs = st_hc[i]
+            ap_ = psum.tile([P, 2, 2 * P], F32, name="ap_", tag="ring")
+            for m in range(2):
+                nc.tensor.matmul_mx(
+                    out=ap_[:, m, :],
+                    lhsT=hc[:, m * P:(m + 1) * P].bitcast(FP8X4),
+                    lhsT_scale=hs[:, m * P:(m + 1) * P],
+                    rhs=hc[:, 2 * P:4 * P].bitcast(FP8X4),
+                    rhs_scale=hs[:, 2 * P:4 * P],
+                    start=True,
+                    stop=True,
+                )
+            st_a[i] = ap_
+
+        def a_evac(i):
+            at = atp.tile([P, 2, 2 * P], F32, name="at", tag="at")
+            o = at[:].rearrange("p m (q j) -> p m q j", j=2)
+            s = st_a[i][:].rearrange("p m (j q) -> p m q j", j=2)
+            if A_ENG == "v":
+                nc.vector.tensor_scalar(out=o, in0=s, scalar1=inv_sqrt_d, scalar2=None, op0=ALU.mult)
+            else:
+                nc.scalar.activation(out=o, in_=s, func=ACT.Copy, scale=inv_sqrt_d)
+            nc.sync.dma_start(out=out_0[i].rearrange("(q m) c -> q m c", m=2), in_=at[:])
+
+        g_f = const.tile([P, 4], F32, name="g_f")
+        nc.vector.tensor_copy(out=g_f[:], in_=g_sb[:])
+        b_f = const.tile([P, 4], F32, name="b_f")
+        nc.vector.tensor_copy(out=b_f[:], in_=b_sb[:])
+        ss = const.tile([P, 4], F32, name="ss")
+        junk = const.tile([P, D], BF16, name="junk")
+        for t in range(4):
+            nc.scalar.activation(out=junk[:], in_=v_sb[:, t, :], func=ACT.Square, accum_out=ss[:, t:t + 1])
+        x_pe(0)
+        x_evac(0, ("v", "v"))
+        nrm = const.tile([P, 4], F32, name="nrm")
+        nc.scalar.activation(out=nrm[:], in_=ss[:], func=ACT.Sqrt)
+        rn = const.tile([P, 4], F32, name="rn")
+        nc.vector.reciprocal(out=rn[:], in_=nrm[:])
+        sc = const.tile([P, 4], F32, name="sc")
+        nc.vector.tensor_tensor(out=sc[:], in0=rn[:], in1=g_f[:], op=ALU.mult)
+        w1b = const.tile([P, 4, D], BF16, name="w1b")
+        for t in range(4):
+            o = w1b[:, t, :].rearrange("p (u e c) -> p u e c", u=2, e=2)
+            s = v_sb[:, t, :].rearrange("p (u c e) -> p u e c", u=2, e=2)
+            if t % 2 == 0:
+                nc.vector.tensor_scalar(out=o, in0=s, scalar1=sc[:, t:t + 1], scalar2=None, op0=ALU.mult)
+            else:
+                nc.scalar.activation(out=o, in_=s, func=ACT.Copy, scale=sc[:, t:t + 1])
+        x_pe(1)
+        wg = const.tile([P, 4 * P, 4], BF16, name="wg", align_bytes=64)
+        wps = []
+        for pr in range(2):
+            wp = psum.tile([P, 2, 4, P], BF16, name="wp", tag="ring")
+            for a in range(2):
+                for tt in range(4):
+                    nc.tensor.transpose(
+                        out=wp[:, a, tt, :], in_=w1b[:, 2 * pr + a, tt * P:(tt + 1) * P], identity=ident_b[:]
+                    )
+            wps.append(wp)
+        x_quant(0)
+        x_evac(1, ("v", "s"))
+        for pr in range(2):
+            evac(
+                "v" if pr == 0 else "s",
+                wg[:, pr * 256:(pr + 1) * 256, :].rearrange("c (a p) t -> c a p t", a=2),
+                wps[pr][:].rearrange("c a t p -> c a p t"),
+            )
+        x_pe(2)
+        x_quant(1)
+        wc = const.tile([P, 4 * P], U32, name="wc", align_bytes=64)
+        ws = const.tile([P, 4 * P], U8, name="ws", align_bytes=64)
+        nc.vector.quantize_mx(out=wc[:].bitcast(FP8X4), scales=ws[:], in_=wg[:].rearrange("c o t -> c (o t)"))
+        nc.scalar.activation(out=dummy2[:], in_=dummy[:], func=ACT.Gelu_apprx_tanh)
+        x_evac(2, ("v", "s"))
+        for r in range(3, LX):
+            x_pe(r)
+            x_evac(r, ("v", "s"))
+            x_quant(r - 1)
+        x_quant(LX - 1)
+
+        for i in range(B):
+            nx = i + LX
+            if i - 3 >= 0:
+                a_evac(i - 3)
+            if nx < B:
+                x_pe(nx)
+                x_evac(nx, ("v", "s") if i == 1 else ("v", "v"))
+            if i - 2 >= 0:
+                h_pe(i - 2)
+                h_evac(i - 2, ("s", "s", "s", "s") if nx < B else ("s", "v", "s", "v"))
+            if i - 1 >= 0:
+                regroup(i - 1)
+            if nx < B:
+                x_quant(nx)
+            if i - 1 >= 0:
+                h_quant(i - 1)
+            z_pe(i)
+            gelu(i)
+            if i - 2 >= 0:
+                a_pe(i - 2)
+        a_evac(B - 3)
+        regroup(B - 1)
+        h_pe(B - 2)
+        h_evac(B - 2, ("s", "s", "s", "s"))
+        h_quant(B - 1)
+        a_pe(B - 2)
+        h_pe(B - 1)
+        a_evac(B - 2)
+        a_pe(B - 1)
+        h_evac(B - 1, ("s", "v", "s", "v"))
+        a_evac(B - 1)

@@ -39,7 +39,8 @@ def tile_mappedattention_pa_t_kernel(tc, head, tail, v1, g1, b1, out_0, out_1, o
         hcp = ctx.enter_context(tc.tile_pool(name="hcp", bufs=3))
         hop = ctx.enter_context(tc.tile_pool(name="hop", bufs=3))
         atp = ctx.enter_context(tc.tile_pool(name="atp", bufs=3))
-        psum = ctx.enter_context(tc.psum_pool(name="psum", bufs=8))
+        psum = ctx.enter_context(tc.psum_pool(name="psum", bufs=7))
+        psa = ctx.enter_context(tc.psum_pool(name="psa", bufs=1))
         if MANUAL:
             ctx.enter_context(tc.manual_schedule())
 
@@ -81,28 +82,27 @@ def tile_mappedattention_pa_t_kernel(tc, head, tail, v1, g1, b1, out_0, out_1, o
         st_hc = {}
         st_hp = {}
         st_a = {}
+        st_ho = {}
 
-        def x_pe(i):
-            banks = []
-            for st in range(2):
-                xp = psum.tile([P, 2, 2, P], F32, name="xp", tag="ring")
-                xw = x_sb[(st, i)][:].bitcast(F32)
-                for j in range(2):
-                    for u in range(2):
-                        off = j * 256 + u * P
-                        nc.tensor.transpose(out=xp[:, j, u, :], in_=xw[:, off:off + P], identity=ident_f[:])
-                banks.append(xp)
-            st_x[i] = banks
+        def x_pe(i, st):
+            xp = psum.tile([P, 2, 2, P], F32, name="xp", tag="ring")
+            xw = x_sb[(st, i)][:].bitcast(F32)
+            for j in range(2):
+                for u in range(2):
+                    off = j * 256 + u * P
+                    nc.tensor.transpose(out=xp[:, j, u, :], in_=xw[:, off:off + P], identity=ident_f[:])
+            st_x[(i, st)] = xp
 
-        def x_evac(i, engs):
-            xg = xgp.tile([P, 4 * P, 2], F32, name="xg", tag="xg", align_bytes=64)
-            for st in range(2):
-                evac(
-                    engs[st],
-                    xg[:, st * 256:(st + 1) * 256, :].rearrange("p (j q) u -> p j q u", j=2),
-                    st_x[i][st][:].rearrange("p j u q -> p j q u"),
-                )
-            st_xg[i] = xg
+        def x_evac(i, st, eng):
+            if st == 0:
+                xg_new = xgp.tile([P, 4 * P, 2], F32, name="xg", tag="xg", align_bytes=64)
+                st_xg[i] = xg_new
+            xg = st_xg[i]
+            evac(
+                eng,
+                xg[:, st * 256:(st + 1) * 256, :].rearrange("p (j q) u -> p j q u", j=2),
+                st_x[(i, st)][:].rearrange("p j u q -> p j q u"),
+            )
 
         def x_quant(i):
             xc = xcp.tile([P, 4 * P], U32, name="xc", tag="xc", align_bytes=64)
@@ -114,31 +114,28 @@ def tile_mappedattention_pa_t_kernel(tc, head, tail, v1, g1, b1, out_0, out_1, o
             )
             st_xc[i] = (xc, xs)
 
-        def z_pe(i):
+        def z_pe(i, t):
             xc, xs = st_xc[i]
-            banks = []
-            for t in range(4):
-                zp = psum.tile([P, 4 * P], F32, name="zp", tag="ring")
-                nc.tensor.matmul_mx(
-                    out=zp[:],
-                    lhsT=wc[:, t * P:(t + 1) * P].bitcast(FP8X4),
-                    lhsT_scale=ws[:, t * P:(t + 1) * P],
-                    rhs=xc[:].bitcast(FP8X4),
-                    rhs_scale=xs[:],
-                    start=True,
-                    stop=True,
-                )
-                banks.append(zp)
-            st_z[i] = banks
+            zp = psum.tile([P, 4 * P], F32, name="zp", tag="ring")
+            nc.tensor.matmul_mx(
+                out=zp[:],
+                lhsT=wc[:, t * P:(t + 1) * P].bitcast(FP8X4),
+                lhsT_scale=ws[:, t * P:(t + 1) * P],
+                rhs=xc[:].bitcast(FP8X4),
+                rhs_scale=xs[:],
+                start=True,
+                stop=True,
+            )
+            st_z[(i, t)] = zp
 
-        def gelu(i):
-            ht = htp.tile([P, 4, 4 * P], F32, name="ht", tag="ht")
-            for t in range(4):
-                nc.scalar.activation(
-                    out=ht[:, t, :], in_=st_z[i][t][:], func=ACT.Gelu_apprx_tanh,
-                    bias=b_f[:, t:t + 1], scale=1.0,
-                )
-            st_ht[i] = ht
+        def gelu(i, t):
+            if t == 0:
+                ht_new = htp.tile([P, 4, 4 * P], F32, name="ht", tag="ht")
+                st_ht[i] = ht_new
+            nc.scalar.activation(
+                out=st_ht[i][:, t, :], in_=st_z[(i, t)][:], func=ACT.Gelu_apprx_tanh,
+                bias=b_f[:, t:t + 1], scale=1.0,
+            )
 
         def regroup(i):
             hg = hgp.tile([P, 4 * P, 4], BF16, name="hg", tag="hg", align_bytes=64)
@@ -155,44 +152,43 @@ def tile_mappedattention_pa_t_kernel(tc, head, tail, v1, g1, b1, out_0, out_1, o
             )
             st_hc[i] = (hc, hs)
 
-        def h_pe(i):
-            banks = []
-            for a in range(4):
-                hp = psum.tile([P, 4, P], F32, name="hp", tag="ring")
-                for t in range(4):
-                    nc.tensor.transpose(out=hp[:, t, :], in_=st_ht[i][:, t, a * P:(a + 1) * P], identity=ident_f[:])
-                banks.append(hp)
-            st_hp[i] = banks
+        def h_pe(i, a):
+            hp = psum.tile([P, 4, P], F32, name="hp", tag="ring")
+            for t in range(4):
+                nc.tensor.transpose(out=hp[:, t, :], in_=st_ht[i][:, t, a * P:(a + 1) * P], identity=ident_f[:])
+            st_hp[(i, a)] = hp
 
-        def h_evac(i, engs):
-            ho = hop.tile([P, 4, D], F32, name="ho", tag="ho")
-            for a in range(4):
-                evac(
-                    engs[a],
-                    ho[:, a, :].rearrange("q (p t) -> q p t", t=4),
-                    st_hp[i][a][:].rearrange("q t p -> q p t"),
+        def h_evac(i, a, eng):
+            if a == 0:
+                ho_new = hop.tile([P, 4, D], F32, name="ho", tag="ho")
+                st_ho[i] = ho_new
+            ho = st_ho[i]
+            evac(
+                eng,
+                ho[:, a, :].rearrange("q (p t) -> q p t", t=4),
+                st_hp[(i, a)][:].rearrange("q t p -> q p t"),
+            )
+            if a % 2 == 1:
+                st = a // 2
+                nc.sync.dma_start(
+                    out=h_outs[st][i].rearrange("(q j) o -> q j o", j=2),
+                    in_=ho[:, 2 * st:2 * st + 2, :],
                 )
-                if a % 2 == 1:
-                    st = a // 2
-                    nc.sync.dma_start(
-                        out=h_outs[st][i].rearrange("(q j) o -> q j o", j=2),
-                        in_=ho[:, 2 * st:2 * st + 2, :],
-                    )
 
-        def a_pe(i):
+        def a_pe(i, m):
             hc, hs = st_hc[i]
-            ap_ = psum.tile([P, 2, 2 * P], F32, name="ap_", tag="ring")
-            for m in range(2):
-                nc.tensor.matmul_mx(
-                    out=ap_[:, m, :],
-                    lhsT=hc[:, m * P:(m + 1) * P].bitcast(FP8X4),
-                    lhsT_scale=hs[:, m * P:(m + 1) * P],
-                    rhs=hc[:, 2 * P:4 * P].bitcast(FP8X4),
-                    rhs_scale=hs[:, 2 * P:4 * P],
-                    start=True,
-                    stop=True,
-                )
-            st_a[i] = ap_
+            if m == 0:
+                a_new = psa.tile([P, 2, 2 * P], F32, name="a_ps", tag="a_ps")
+                st_a[i] = a_new
+            nc.tensor.matmul_mx(
+                out=st_a[i][:, m, :],
+                lhsT=hc[:, m * P:(m + 1) * P].bitcast(FP8X4),
+                lhsT_scale=hs[:, m * P:(m + 1) * P],
+                rhs=hc[:, 2 * P:4 * P].bitcast(FP8X4),
+                rhs_scale=hs[:, 2 * P:4 * P],
+                start=True,
+                stop=True,
+            )
 
         def a_evac(i):
             at = atp.tile([P, 2, 2 * P], F32, name="at", tag="at")
@@ -212,8 +208,10 @@ def tile_mappedattention_pa_t_kernel(tc, head, tail, v1, g1, b1, out_0, out_1, o
         junk = const.tile([P, D], BF16, name="junk")
         for t in range(4):
             nc.scalar.activation(out=junk[:], in_=v_sb[:, t, :], func=ACT.Square, accum_out=ss[:, t:t + 1])
-        x_pe(0)
-        x_evac(0, ("v", "v"))
+        x_pe(0, 0)
+        x_pe(0, 1)
+        x_evac(0, 0, "v")
+        x_evac(0, 1, "v")
         nrm = const.tile([P, 4], F32, name="nrm")
         nc.scalar.activation(out=nrm[:], in_=ss[:], func=ACT.Sqrt)
         rn = const.tile([P, 4], F32, name="rn")
@@ -228,7 +226,8 @@ def tile_mappedattention_pa_t_kernel(tc, head, tail, v1, g1, b1, out_0, out_1, o
                 nc.vector.tensor_scalar(out=o, in0=s, scalar1=sc[:, t:t + 1], scalar2=None, op0=ALU.mult)
             else:
                 nc.scalar.activation(out=o, in_=s, func=ACT.Copy, scale=sc[:, t:t + 1])
-        x_pe(1)
+        x_pe(1, 0)
+        x_pe(1, 1)
         wg = const.tile([P, 4 * P, 4], BF16, name="wg", align_bytes=64)
         wps = []
         for pr in range(2):
@@ -240,54 +239,72 @@ def tile_mappedattention_pa_t_kernel(tc, head, tail, v1, g1, b1, out_0, out_1, o
                     )
             wps.append(wp)
         x_quant(0)
-        x_evac(1, ("v", "s"))
+        x_evac(1, 0, "v")
+        x_evac(1, 1, "s")
         for pr in range(2):
             evac(
                 "v" if pr == 0 else "s",
                 wg[:, pr * 256:(pr + 1) * 256, :].rearrange("c (a p) t -> c a p t", a=2),
                 wps[pr][:].rearrange("c a t p -> c a p t"),
             )
-        x_pe(2)
+        x_pe(2, 0)
+        x_pe(2, 1)
         x_quant(1)
         wc = const.tile([P, 4 * P], U32, name="wc", align_bytes=64)
         ws = const.tile([P, 4 * P], U8, name="ws", align_bytes=64)
         nc.vector.quantize_mx(out=wc[:].bitcast(FP8X4), scales=ws[:], in_=wg[:].rearrange("c o t -> c (o t)"))
         nc.scalar.activation(out=dummy2[:], in_=dummy[:], func=ACT.Gelu_apprx_tanh)
-        x_evac(2, ("v", "s"))
+        x_evac(2, 0, "v")
+        x_evac(2, 1, "s")
         for r in range(3, LX):
-            x_pe(r)
-            x_evac(r, ("v", "s"))
+            x_pe(r, 0)
+            x_pe(r, 1)
+            x_evac(r, 0, "v")
+            x_evac(r, 1, "s")
             x_quant(r - 1)
         x_quant(LX - 1)
 
         for i in range(B):
             nx = i + LX
+            he = ("s", "s", "s", "s") if nx < B else ("s", "v", "s", "v")
             if i - 3 >= 0:
                 a_evac(i - 3)
-            if nx < B:
-                x_pe(nx)
-                x_evac(nx, ("v", "s") if i == 1 else ("v", "v"))
-            if i - 2 >= 0:
-                h_pe(i - 2)
-                h_evac(i - 2, ("s", "s", "s", "s") if nx < B else ("s", "v", "s", "v"))
-            if i - 1 >= 0:
-                regroup(i - 1)
-            if nx < B:
-                x_quant(nx)
-            if i - 1 >= 0:
-                h_quant(i - 1)
-            z_pe(i)
-            gelu(i)
-            if i - 2 >= 0:
-                a_pe(i - 2)
+            for half in range(2):
+                if nx < B:
+                    x_pe(nx, half)
+                    x_evac(nx, half, "s" if (i == 1 and half == 1) else "v")
+                if i - 2 >= 0:
+                    for a in (2 * half, 2 * half + 1):
+                        h_pe(i - 2, a)
+                    for a in (2 * half, 2 * half + 1):
+                        h_evac(i - 2, a, he[a])
+                if half == 0 and i - 1 >= 0:
+                    regroup(i - 1)
+                if half == 1:
+                    if i - 1 >= 0:
+                        h_quant(i - 1)
+                    if nx < B:
+                        x_quant(nx)
+                for t in (2 * half, 2 * half + 1):
+                    z_pe(i, t)
+                for t in (2 * half, 2 * half + 1):
+                    gelu(i, t)
+                if i - 2 >= 0:
+                    a_pe(i - 2, half)
         a_evac(B - 3)
         regroup(B - 1)
-        h_pe(B - 2)
-        h_evac(B - 2, ("s", "s", "s", "s"))
+        for a in range(4):
+            h_pe(B - 2, a)
+        for a in range(4):
+            h_evac(B - 2, a, "s")
         h_quant(B - 1)
-        a_pe(B - 2)
-        h_pe(B - 1)
+        a_pe(B - 2, 0)
+        a_pe(B - 2, 1)
+        for a in range(4):
+            h_pe(B - 1, a)
         a_evac(B - 2)
-        a_pe(B - 1)
-        h_evac(B - 1, ("s", "v", "s", "v"))
+        a_pe(B - 1, 0)
+        a_pe(B - 1, 1)
+        for a in range(4):
+            h_evac(B - 1, a, ("s", "v", "s", "v")[a])
         a_evac(B - 1)

@@ -139,7 +139,10 @@ def tile_mappedattention_pa_t_kernel(tc, head, tail, v1, g1, b1, out_0, out_1, o
 
         def regroup(i):
             hg = hgp.tile([P, 4 * P, 4], BF16, name="hg", tag="hg", align_bytes=64)
-            nc.vector.tensor_copy(out=hg[:], in_=st_ht[i][:].rearrange("p t c -> p c t"))
+            nc.vector.tensor_copy(
+                out=hg[:].rearrange("p (c i) t -> p c t i", i=4),
+                in_=st_ht[i][:].rearrange("p t (c i) -> p c t i", i=4),
+            )
             st_hg[i] = hg
 
         def h_quant(i):

@@ -20,7 +20,6 @@ FLOPS = 2 * (2 * B * S) * D * D + 2 * B * S * S * D
 
 MANUAL = True
 LX = 4
-A_ENG = "v"
 
 
 def tile_mappedattention_pa_t_kernel(tc, head, tail, v1, g1, b1, out_0, out_1, out_2):
@@ -34,13 +33,13 @@ def tile_mappedattention_pa_t_kernel(tc, head, tail, v1, g1, b1, out_0, out_1, o
         xin = ctx.enter_context(tc.tile_pool(name="xin", bufs=1))
         xgp = ctx.enter_context(tc.tile_pool(name="xgp", bufs=3))
         xcp = ctx.enter_context(tc.tile_pool(name="xcp", bufs=LX + 2))
-        htp = ctx.enter_context(tc.tile_pool(name="htp", bufs=3))
+        htp = ctx.enter_context(tc.tile_pool(name="htp", bufs=4))
         hgp = ctx.enter_context(tc.tile_pool(name="hgp", bufs=2))
-        hcp = ctx.enter_context(tc.tile_pool(name="hcp", bufs=3))
+        hcp = ctx.enter_context(tc.tile_pool(name="hcp", bufs=4))
         hop = ctx.enter_context(tc.tile_pool(name="hop", bufs=3))
         atp = ctx.enter_context(tc.tile_pool(name="atp", bufs=3))
-        psum = ctx.enter_context(tc.psum_pool(name="psum", bufs=7))
-        psa = ctx.enter_context(tc.psum_pool(name="psa", bufs=1))
+        psum = ctx.enter_context(tc.psum_pool(name="psum", bufs=6))
+        psa = ctx.enter_context(tc.psum_pool(name="psa", bufs=2))
         if MANUAL:
             ctx.enter_context(tc.manual_schedule())
 
@@ -193,11 +192,11 @@ def tile_mappedattention_pa_t_kernel(tc, head, tail, v1, g1, b1, out_0, out_1, o
                 stop=True,
             )
 
-        def a_evac(i):
+        def a_evac(i, eng):
             at = atp.tile([P, 2, 2 * P], F32, name="at", tag="at")
             o = at[:].rearrange("p m (q j) -> p m q j", j=2)
             s = st_a[i][:].rearrange("p m (j q) -> p m q j", j=2)
-            if A_ENG == "v":
+            if eng == "v":
                 nc.vector.tensor_scalar(out=o, in0=s, scalar1=inv_sqrt_d, scalar2=None, op0=ALU.mult)
             else:
                 nc.scalar.activation(out=o, in_=s, func=ACT.Copy, scale=inv_sqrt_d)
@@ -267,47 +266,44 @@ def tile_mappedattention_pa_t_kernel(tc, head, tail, v1, g1, b1, out_0, out_1, o
             x_quant(r - 1)
         x_quant(LX - 1)
 
-        for i in range(B):
+        turn = [0]
+
+        def pick(kind, i, k):
+            if i + LX < B:
+                turn[0] += 1
+                return "v" if turn[0] % 2 == 1 else "s"
+            if i < B:
+                return "v" if (kind == "a" or k % 2 == 0) else "s"
+            if i == B:
+                return "v" if (kind == "a" or k == 0) else "s"
+            if i == B + 1:
+                return "s" if (kind == "a" or k % 2 == 1) else "v"
+            return "v" if i == B + 2 else "s"
+
+        for i in range(B + 4):
             nx = i + LX
-            he = ("s", "s", "s", "s") if nx < B else ("s", "v", "s", "v")
-            if i - 3 >= 0:
-                a_evac(i - 3)
+            if 0 <= i - 4 < B:
+                a_evac(i - 4, pick("a", i, 0))
             for half in range(2):
                 if nx < B:
                     x_pe(nx, half)
-                    x_evac(nx, half, "s" if (i == 1 and half == 1) else "v")
-                if i - 2 >= 0:
+                    x_evac(nx, half, pick("x", i, half))
+                if 0 <= i - 2 < B:
                     for a in (2 * half, 2 * half + 1):
                         h_pe(i - 2, a)
                     for a in (2 * half, 2 * half + 1):
-                        h_evac(i - 2, a, he[a])
-                if half == 0 and i - 1 >= 0:
+                        h_evac(i - 2, a, pick("h", i, a))
+                if half == 0 and 0 <= i - 1 < B:
                     regroup(i - 1)
                 if half == 1:
-                    if i - 1 >= 0:
+                    if 0 <= i - 1 < B:
                         h_quant(i - 1)
                     if nx < B:
                         x_quant(nx)
-                for t in (2 * half, 2 * half + 1):
-                    z_pe(i, t)
-                for t in (2 * half, 2 * half + 1):
-                    gelu(i, t)
-                if i - 2 >= 0:
-                    a_pe(i - 2, half)
-        a_evac(B - 3)
-        regroup(B - 1)
-        for a in range(4):
-            h_pe(B - 2, a)
-        for a in range(4):
-            h_evac(B - 2, a, "s")
-        h_quant(B - 1)
-        a_pe(B - 2, 0)
-        a_pe(B - 2, 1)
-        for a in range(4):
-            h_pe(B - 1, a)
-        a_evac(B - 2)
-        a_pe(B - 1, 0)
-        a_pe(B - 1, 1)
-        for a in range(4):
-            h_evac(B - 1, a, ("s", "v", "s", "v")[a])
-        a_evac(B - 1)
+                if i < B:
+                    for t in (2 * half, 2 * half + 1):
+                        z_pe(i, t)
+                    for t in (2 * half, 2 * half + 1):
+                        gelu(i, t)
+                if 0 <= i - 3 < B:
+                    a_pe(i - 3, half)

@@ -20,6 +20,7 @@ FLOPS = 2 * (2 * B * S) * D * D + 2 * B * S * S * D
 
 MANUAL = True
 LX = 4
+A_ENG = "v"
 
 
 def tile_mappedattention_pa_t_kernel(tc, head, tail, v1, g1, b1, out_0, out_1, out_2):
@@ -33,13 +34,13 @@ def tile_mappedattention_pa_t_kernel(tc, head, tail, v1, g1, b1, out_0, out_1, o
         xin = ctx.enter_context(tc.tile_pool(name="xin", bufs=1))
         xgp = ctx.enter_context(tc.tile_pool(name="xgp", bufs=3))
         xcp = ctx.enter_context(tc.tile_pool(name="xcp", bufs=LX + 2))
-        htp = ctx.enter_context(tc.tile_pool(name="htp", bufs=4))
+        htp = ctx.enter_context(tc.tile_pool(name="htp", bufs=3))
         hgp = ctx.enter_context(tc.tile_pool(name="hgp", bufs=2))
-        hcp = ctx.enter_context(tc.tile_pool(name="hcp", bufs=4))
+        hcp = ctx.enter_context(tc.tile_pool(name="hcp", bufs=3))
         hop = ctx.enter_context(tc.tile_pool(name="hop", bufs=3))
         atp = ctx.enter_context(tc.tile_pool(name="atp", bufs=3))
-        psum = ctx.enter_context(tc.psum_pool(name="psum", bufs=6))
-        psa = ctx.enter_context(tc.psum_pool(name="psa", bufs=2))
+        psum = ctx.enter_context(tc.psum_pool(name="psum", bufs=7))
+        psa = ctx.enter_context(tc.psum_pool(name="psa", bufs=1))
         if MANUAL:
             ctx.enter_context(tc.manual_schedule())
 
@@ -192,42 +193,45 @@ def tile_mappedattention_pa_t_kernel(tc, head, tail, v1, g1, b1, out_0, out_1, o
                 stop=True,
             )
 
-        def a_evac(i, eng):
+        def a_evac(i):
             at = atp.tile([P, 2, 2 * P], F32, name="at", tag="at")
             o = at[:].rearrange("p m (q j) -> p m q j", j=2)
             s = st_a[i][:].rearrange("p m (j q) -> p m q j", j=2)
-            if eng == "v":
+            if A_ENG == "v":
                 nc.vector.tensor_scalar(out=o, in0=s, scalar1=inv_sqrt_d, scalar2=None, op0=ALU.mult)
             else:
                 nc.scalar.activation(out=o, in_=s, func=ACT.Copy, scale=inv_sqrt_d)
             nc.sync.dma_start(out=out_0[i].rearrange("(q m) c -> q m c", m=2), in_=at[:])
 
+        ss = const.tile([P, 4, 8], F32, name="ss")
+        junk = const.tile([P, D], BF16, name="junk")
+        for t in range(3):
+            nc.scalar.activation(out=junk[:], in_=v_sb[:, t, :], func=ACT.Square, accum_out=ss[:, t, 0:1])
+        sq3 = const.tile([P, D], F32, name="sq3")
+        nc.vector.tensor_tensor(out=sq3[:], in0=v_sb[:, 3, :], in1=v_sb[:, 3, :], op=ALU.mult)
+        nc.vector.tensor_reduce(out=ss[:, 3, 0:1], in_=sq3[:], axis=mybir.AxisListType.X, op=ALU.add)
         g_f = const.tile([P, 4], F32, name="g_f")
         nc.vector.tensor_copy(out=g_f[:], in_=g_sb[:])
         b_f = const.tile([P, 4], F32, name="b_f")
         nc.vector.tensor_copy(out=b_f[:], in_=b_sb[:])
-        ss = const.tile([P, 4], F32, name="ss")
-        junk = const.tile([P, D], BF16, name="junk")
-        for t in range(4):
-            nc.scalar.activation(out=junk[:], in_=v_sb[:, t, :], func=ACT.Square, accum_out=ss[:, t:t + 1])
         x_pe(0, 0)
         x_pe(0, 1)
         x_evac(0, 0, "v")
         x_evac(0, 1, "v")
         nrm = const.tile([P, 4], F32, name="nrm")
-        nc.scalar.activation(out=nrm[:], in_=ss[:], func=ACT.Sqrt)
+        nc.scalar.activation(out=nrm[:], in_=ss[:, :, 0], func=ACT.Sqrt)
+        nc.scalar.activation(out=dummy2[:], in_=dummy[:], func=ACT.Gelu_apprx_tanh)
         rn = const.tile([P, 4], F32, name="rn")
         nc.vector.reciprocal(out=rn[:], in_=nrm[:])
         sc = const.tile([P, 4], F32, name="sc")
         nc.vector.tensor_tensor(out=sc[:], in0=rn[:], in1=g_f[:], op=ALU.mult)
         w1b = const.tile([P, 4, D], BF16, name="w1b")
         for t in range(4):
-            o = w1b[:, t, :].rearrange("p (u e c) -> p u e c", u=2, e=2)
-            s = v_sb[:, t, :].rearrange("p (u c e) -> p u e c", u=2, e=2)
-            if t % 2 == 0:
-                nc.vector.tensor_scalar(out=o, in0=s, scalar1=sc[:, t:t + 1], scalar2=None, op0=ALU.mult)
-            else:
-                nc.scalar.activation(out=o, in_=s, func=ACT.Copy, scale=sc[:, t:t + 1])
+            nc.vector.tensor_scalar(
+                out=w1b[:, t, :].rearrange("p (u e c) -> p u e c", u=2, e=2),
+                in0=v_sb[:, t, :].rearrange("p (u c e) -> p u e c", u=2, e=2),
+                scalar1=sc[:, t:t + 1], scalar2=None, op0=ALU.mult,
+            )
         x_pe(1, 0)
         x_pe(1, 1)
         wg = const.tile([P, 4 * P, 4], BF16, name="wg", align_bytes=64)
@@ -240,9 +244,9 @@ def tile_mappedattention_pa_t_kernel(tc, head, tail, v1, g1, b1, out_0, out_1, o
                         out=wp[:, a, tt, :], in_=w1b[:, 2 * pr + a, tt * P:(tt + 1) * P], identity=ident_b[:]
                     )
             wps.append(wp)
-        x_quant(0)
-        x_evac(1, 0, "v")
+        x_evac(1, 0, "s")
         x_evac(1, 1, "s")
+        x_quant(0)
         for pr in range(2):
             evac(
                 "v" if pr == 0 else "s",
@@ -255,7 +259,6 @@ def tile_mappedattention_pa_t_kernel(tc, head, tail, v1, g1, b1, out_0, out_1, o
         wc = const.tile([P, 4 * P], U32, name="wc", align_bytes=64)
         ws = const.tile([P, 4 * P], U8, name="ws", align_bytes=64)
         nc.vector.quantize_mx(out=wc[:].bitcast(FP8X4), scales=ws[:], in_=wg[:].rearrange("c o t -> c (o t)"))
-        nc.scalar.activation(out=dummy2[:], in_=dummy[:], func=ACT.Gelu_apprx_tanh)
         x_evac(2, 0, "v")
         x_evac(2, 1, "s")
         for r in range(3, LX):
@@ -266,44 +269,47 @@ def tile_mappedattention_pa_t_kernel(tc, head, tail, v1, g1, b1, out_0, out_1, o
             x_quant(r - 1)
         x_quant(LX - 1)
 
-        turn = [0]
-
-        def pick(kind, i, k):
-            if i + LX < B:
-                turn[0] += 1
-                return "v" if turn[0] % 2 == 1 else "s"
-            if i < B:
-                return "v" if (kind == "a" or k % 2 == 0) else "s"
-            if i == B:
-                return "v" if (kind == "a" or k == 0) else "s"
-            if i == B + 1:
-                return "s" if (kind == "a" or k % 2 == 1) else "v"
-            return "v" if i == B + 2 else "s"
-
-        for i in range(B + 4):
+        for i in range(B):
             nx = i + LX
-            if 0 <= i - 4 < B:
-                a_evac(i - 4, pick("a", i, 0))
+            he = ("s", "s", "s", "s") if nx < B else ("s", "v", "s", "v")
+            if i - 3 >= 0:
+                a_evac(i - 3)
             for half in range(2):
                 if nx < B:
                     x_pe(nx, half)
-                    x_evac(nx, half, pick("x", i, half))
-                if 0 <= i - 2 < B:
+                    x_evac(nx, half, "s" if (i == 1 and half == 1) else "v")
+                if i - 2 >= 0:
                     for a in (2 * half, 2 * half + 1):
                         h_pe(i - 2, a)
                     for a in (2 * half, 2 * half + 1):
-                        h_evac(i - 2, a, pick("h", i, a))
-                if half == 0 and 0 <= i - 1 < B:
+                        h_evac(i - 2, a, he[a])
+                if half == 0 and i - 1 >= 0:
                     regroup(i - 1)
                 if half == 1:
-                    if 0 <= i - 1 < B:
+                    if i - 1 >= 0:
                         h_quant(i - 1)
                     if nx < B:
                         x_quant(nx)
-                if i < B:
-                    for t in (2 * half, 2 * half + 1):
-                        z_pe(i, t)
-                    for t in (2 * half, 2 * half + 1):
-                        gelu(i, t)
-                if 0 <= i - 3 < B:
-                    a_pe(i - 3, half)
+                for t in (2 * half, 2 * half + 1):
+                    z_pe(i, t)
+                for t in (2 * half, 2 * half + 1):
+                    gelu(i, t)
+                if i - 2 >= 0:
+                    a_pe(i - 2, half)
+        a_evac(B - 3)
+        regroup(B - 1)
+        for a in range(4):
+            h_pe(B - 2, a)
+        for a in range(4):
+            h_evac(B - 2, a, "s")
+        h_quant(B - 1)
+        a_pe(B - 2, 0)
+        a_pe(B - 2, 1)
+        for a in range(4):
+            h_pe(B - 1, a)
+        a_evac(B - 2)
+        a_pe(B - 1, 0)
+        a_pe(B - 1, 1)
+        for a in range(4):
+            h_evac(B - 1, a, ("s", "s", "v", "s")[a])
+        a_evac(B - 1)

@@ -51,7 +51,9 @@ def tile_mappedattention_pa_t_kernel(tc, head, tail, v1, g1, b1, out_0, out_1, o
                 nc.scalar.copy(out=out, in_=in_)
 
         v_sb = const.tile([P, 4, D], BF16, name="v_sb")
-        nc.sync.dma_start(out=v_sb[:], in_=v1.rearrange("(p t) k -> p t k", t=4))
+        v_rows = v1.rearrange("(p t) k -> p t k", t=4)
+        for t in range(4):
+            nc.sync.dma_start(out=v_sb[:, t, :], in_=v_rows[:, t, :])
         g_sb = const.tile([P, 4], BF16, name="g_sb")
         b_sb = const.tile([P, 4], BF16, name="b_sb")
         with nc.allow_non_contiguous_dma(reason="four bf16 values to a partition"):
@@ -214,10 +216,6 @@ def tile_mappedattention_pa_t_kernel(tc, head, tail, v1, g1, b1, out_0, out_1, o
         nc.vector.tensor_copy(out=g_f[:], in_=g_sb[:])
         b_f = const.tile([P, 4], F32, name="b_f")
         nc.vector.tensor_copy(out=b_f[:], in_=b_sb[:])
-        x_pe(0, 0)
-        x_pe(0, 1)
-        x_evac(0, 0, "v")
-        x_evac(0, 1, "v")
         nrm = const.tile([P, 4], F32, name="nrm")
         nc.scalar.activation(out=nrm[:], in_=ss[:, :, 0], func=ACT.Sqrt)
         nc.scalar.activation(out=dummy2[:], in_=dummy[:], func=ACT.Gelu_apprx_tanh)
@@ -232,6 +230,8 @@ def tile_mappedattention_pa_t_kernel(tc, head, tail, v1, g1, b1, out_0, out_1, o
                 in0=v_sb[:, t, :].rearrange("p (u c e) -> p u e c", u=2, e=2),
                 scalar1=sc[:, t:t + 1], scalar2=None, op0=ALU.mult,
             )
+        x_pe(0, 0)
+        x_pe(0, 1)
         x_pe(1, 0)
         x_pe(1, 1)
         wg = const.tile([P, 4 * P, 4], BF16, name="wg", align_bytes=64)
@@ -244,6 +244,8 @@ def tile_mappedattention_pa_t_kernel(tc, head, tail, v1, g1, b1, out_0, out_1, o
                         out=wp[:, a, tt, :], in_=w1b[:, 2 * pr + a, tt * P:(tt + 1) * P], identity=ident_b[:]
                     )
             wps.append(wp)
+        x_evac(0, 0, "v")
+        x_evac(0, 1, "s")
         x_evac(1, 0, "s")
         x_evac(1, 1, "s")
         x_quant(0)
@@ -271,7 +273,12 @@ def tile_mappedattention_pa_t_kernel(tc, head, tail, v1, g1, b1, out_0, out_1, o
 
         for i in range(B):
             nx = i + LX
-            he = ("s", "s", "s", "s") if nx < B else ("s", "v", "s", "v")
+            if nx >= B:
+                he = ("s", "v", "s", "v")
+            elif i % 4 == 0:
+                he = ("s", "s", "s", "v")
+            else:
+                he = ("s", "s", "s", "s")
             if i - 3 >= 0:
                 a_evac(i - 3)
             for half in range(2):

@@ -66,14 +66,14 @@ def tile_mappedattention_pa_t_kernel(tc, head, tail, v1, g1, b1, out_0, out_1, o
                 nc.sync.dma_start(out=xt[:], in_=streams[st][b].rearrange("(q j) k -> q (j k)", j=2))
                 x_sb[(st, b)] = xt
 
-        ident_f = const.tile([P, P], F32, name="ident_f")
-        make_identity(nc, ident_f[:])
-        ident_b = const.tile([P, P], BF16, name="ident_b")
-        make_identity(nc, ident_b[:])
         dummy = const.tile([P, 1], F32, name="dummy")
         nc.vector.memset(dummy[:], 1.0)
         dummy2 = const.tile([P, 1], F32, name="dummy2")
-        nc.scalar.activation(out=dummy2[:], in_=dummy[:], func=ACT.Sqrt)
+        nc.scalar.activation(out=dummy2[:], in_=dummy[:], func=ACT.Gelu_apprx_tanh)
+        ident_f = const.tile([P, P], F32, name="ident_f")
+        make_identity(nc, ident_f[:])
+        minus_half = const.tile([P, 4], F32, name="minus_half")
+        nc.gpsimd.memset(minus_half[:], -0.5)
 
         st_x = {}
         st_xg = {}
@@ -136,7 +136,7 @@ def tile_mappedattention_pa_t_kernel(tc, head, tail, v1, g1, b1, out_0, out_1, o
                 st_ht[i] = ht_new
             nc.scalar.activation(
                 out=st_ht[i][:, t, :], in_=st_z[(i, t)][:], func=ACT.Gelu_apprx_tanh,
-                bias=b_f[:, t:t + 1], scale=1.0,
+                bias=b_sb[:, t:t + 1], scale=1.0,
             )
 
         def regroup(i):
@@ -205,71 +205,61 @@ def tile_mappedattention_pa_t_kernel(tc, head, tail, v1, g1, b1, out_0, out_1, o
                 nc.scalar.activation(out=o, in_=s, func=ACT.Copy, scale=inv_sqrt_d)
             nc.sync.dma_start(out=out_0[i].rearrange("(q m) c -> q m c", m=2), in_=at[:])
 
-        ss = const.tile([P, 4, 8], F32, name="ss")
-        junk = const.tile([P, D], BF16, name="junk")
-        for t in range(3):
-            nc.scalar.activation(out=junk[:], in_=v_sb[:, t, :], func=ACT.Square, accum_out=ss[:, t, 0:1])
-        sq3 = const.tile([P, D], F32, name="sq3")
-        nc.vector.tensor_tensor(out=sq3[:], in0=v_sb[:, 3, :], in1=v_sb[:, 3, :], op=ALU.mult)
-        nc.vector.tensor_reduce(out=ss[:, 3, 0:1], in_=sq3[:], axis=mybir.AxisListType.X, op=ALU.add)
-        g_f = const.tile([P, 4], F32, name="g_f")
-        nc.vector.tensor_copy(out=g_f[:], in_=g_sb[:])
-        b_f = const.tile([P, 4], F32, name="b_f")
-        nc.vector.tensor_copy(out=b_f[:], in_=b_sb[:])
-        nrm = const.tile([P, 4], F32, name="nrm")
-        nc.scalar.activation(out=nrm[:], in_=ss[:, :, 0], func=ACT.Sqrt)
-        nc.scalar.activation(out=dummy2[:], in_=dummy[:], func=ACT.Gelu_apprx_tanh)
-        rn = const.tile([P, 4], F32, name="rn")
-        nc.vector.reciprocal(out=rn[:], in_=nrm[:])
-        sc = const.tile([P, 4], F32, name="sc")
-        nc.vector.tensor_tensor(out=sc[:], in0=rn[:], in1=g_f[:], op=ALU.mult)
-        w1b = const.tile([P, 4, D], BF16, name="w1b")
-        for t in range(4):
-            nc.vector.tensor_scalar(
-                out=w1b[:, t, :].rearrange("p (u e c) -> p u e c", u=2, e=2),
-                in0=v_sb[:, t, :].rearrange("p (u c e) -> p u e c", u=2, e=2),
-                scalar1=sc[:, t:t + 1], scalar2=None, op0=ALU.mult,
+        ss = const.tile([P, 4], F32, name="ss")
+        junk_s = const.tile([P, D], BF16, name="junk_s")
+        junk_v = const.tile([P, D], BF16, name="junk_v")
+        for t in (0, 2):
+            nc.scalar.activation(out=junk_s[:], in_=v_sb[:, t, :], func=ACT.Square, accum_out=ss[:, t:t + 1])
+            nc.vector.scalar_tensor_tensor(
+                out=junk_v[:], in0=v_sb[:, t + 1, :], scalar=1.0, in1=v_sb[:, t + 1, :],
+                op0=ALU.mult, op1=ALU.mult, accum_out=ss[:, t + 1:t + 2],
             )
+        rn = const.tile([P, 4], F32, name="rn")
+        nc.gpsimd.tensor_tensor(out=rn[:], in0=ss[:], in1=minus_half[:], op=ALU.pow)
+        sc = const.tile([P, 4], F32, name="sc")
+        nc.gpsimd.tensor_tensor(out=sc[:], in0=rn[:], in1=g_sb[:], op=ALU.mult)
         x_pe(0, 0)
         x_pe(0, 1)
         x_pe(1, 0)
         x_pe(1, 1)
-        wg = const.tile([P, 4 * P, 4], BF16, name="wg", align_bytes=64)
-        wps = []
-        for pr in range(2):
-            wp = psum.tile([P, 2, 4, P], BF16, name="wp", tag="ring")
-            for a in range(2):
-                for tt in range(4):
-                    nc.tensor.transpose(
-                        out=wp[:, a, tt, :], in_=w1b[:, 2 * pr + a, tt * P:(tt + 1) * P], identity=ident_b[:]
-                    )
-            wps.append(wp)
         x_evac(0, 0, "v")
         x_evac(0, 1, "s")
         x_evac(1, 0, "s")
-        x_evac(1, 1, "s")
+        w1b = const.tile([P, 4, D], BF16, name="w1b")
+        for t in range(4):
+            nc.vector.tensor_scalar(
+                out=w1b[:, t, :], in0=v_sb[:, t, :], scalar1=sc[:, t:t + 1], scalar2=None, op0=ALU.mult,
+            )
+        wg = const.tile([P, 4 * P, 2], F32, name="wg", align_bytes=64)
+        wps = []
+        for pr in range(2):
+            wp = psum.tile([P, 2, 2, P], F32, name="wp", tag="ring")
+            for a in range(2):
+                ww = w1b[:, 2 * pr + a, :].bitcast(F32)
+                for u in range(2):
+                    nc.tensor.transpose(out=wp[:, a, u, :], in_=ww[:, u * P:(u + 1) * P], identity=ident_f[:])
+            wps.append(wp)
         x_quant(0)
         for pr in range(2):
             evac(
                 "v" if pr == 0 else "s",
-                wg[:, pr * 256:(pr + 1) * 256, :].rearrange("c (a p) t -> c a p t", a=2),
-                wps[pr][:].rearrange("c a t p -> c a p t"),
+                wg[:, pr * 256:(pr + 1) * 256, :].rearrange("c (a p) u -> c a p u", a=2),
+                wps[pr][:].rearrange("c a u p -> c a p u"),
             )
+        x_evac(1, 1, "s")
         x_pe(2, 0)
         x_pe(2, 1)
-        x_quant(1)
         wc = const.tile([P, 4 * P], U32, name="wc", align_bytes=64)
         ws = const.tile([P, 4 * P], U8, name="ws", align_bytes=64)
-        nc.vector.quantize_mx(out=wc[:].bitcast(FP8X4), scales=ws[:], in_=wg[:].rearrange("c o t -> c (o t)"))
+        nc.vector.quantize_mx(
+            out=wc[:].bitcast(FP8X4), scales=ws[:], in_=wg[:].rearrange("c o u -> c (o u)").bitcast(BF16)
+        )
+        x_quant(1)
         x_evac(2, 0, "v")
         x_evac(2, 1, "s")
-        for r in range(3, LX):
-            x_pe(r, 0)
-            x_pe(r, 1)
-            x_evac(r, 0, "v")
-            x_evac(r, 1, "s")
-            x_quant(r - 1)
-        x_quant(LX - 1)
+        x_pe(3, 0)
+        x_pe(3, 1)
+        x_quant(2)
 
         for i in range(B):
             nx = i + LX
@@ -282,6 +272,10 @@ def tile_mappedattention_pa_t_kernel(tc, head, tail, v1, g1, b1, out_0, out_1, o
             if i - 3 >= 0:
                 a_evac(i - 3)
             for half in range(2):
+                if i == 0:
+                    x_evac(LX - 1, half, "s")
+                    if half == 1:
+                        x_quant(LX - 1)
                 if nx < B:
                     x_pe(nx, half)
                     x_evac(nx, half, "s" if (i == 1 and half == 1) else "v")

@@ -18,9 +18,9 @@ P = 128
 B, S, D = 16, 256, 512
 FLOPS = 2 * (2 * B * S) * D * D + 2 * B * S * S * D
 
-MANUAL = True
+HE = (("s", "v", "s", "s"), ("s", "s", "s", "s"))
+HLATE = ("s", "v", "v", "s")
 LX = 4
-A_ENG = "v"
 
 
 def tile_mappedattention_pa_t_kernel(tc, head, tail, v1, g1, b1, out_0, out_1, out_2):
@@ -33,7 +33,7 @@ def tile_mappedattention_pa_t_kernel(tc, head, tail, v1, g1, b1, out_0, out_1, o
         const = ctx.enter_context(tc.tile_pool(name="const", bufs=1))
         xin = ctx.enter_context(tc.tile_pool(name="xin", bufs=1))
         xgp = ctx.enter_context(tc.tile_pool(name="xgp", bufs=3))
-        xcp = ctx.enter_context(tc.tile_pool(name="xcp", bufs=LX + 2))
+        xcp = ctx.enter_context(tc.tile_pool(name="xcp", bufs=7))
         htp = ctx.enter_context(tc.tile_pool(name="htp", bufs=3))
         hgp = ctx.enter_context(tc.tile_pool(name="hgp", bufs=2))
         hcp = ctx.enter_context(tc.tile_pool(name="hcp", bufs=3))
@@ -41,8 +41,7 @@ def tile_mappedattention_pa_t_kernel(tc, head, tail, v1, g1, b1, out_0, out_1, o
         atp = ctx.enter_context(tc.tile_pool(name="atp", bufs=3))
         psum = ctx.enter_context(tc.psum_pool(name="psum", bufs=7))
         psa = ctx.enter_context(tc.psum_pool(name="psa", bufs=1))
-        if MANUAL:
-            ctx.enter_context(tc.manual_schedule())
+        ctx.enter_context(tc.manual_schedule())
 
         def evac(eng, out, in_):
             if eng == "v":
@@ -65,6 +64,14 @@ def tile_mappedattention_pa_t_kernel(tc, head, tail, v1, g1, b1, out_0, out_1, o
                 xt = xin.tile([P, 2 * D], BF16, name="x%d_%d" % (st, b))
                 nc.sync.dma_start(out=xt[:], in_=streams[st][b].rearrange("(q j) k -> q (j k)", j=2))
                 x_sb[(st, b)] = xt
+
+        warm = const.tile([P, D], BF16, name="warm")
+        nc.vector.memset(warm[:], 0.0)
+
+        def warm_pe(n):
+            wm = psa.tile([P, 2, 2 * P], F32, name="wm", tag="a_ps")
+            for k in range(n):
+                nc.tensor.matmul(out=wm[:].rearrange("p m c -> p (m c)"), lhsT=warm[:, 0:P], rhs=warm[:], start=True, stop=True)
 
         dummy = const.tile([P, 1], F32, name="dummy")
         nc.vector.memset(dummy[:], 1.0)
@@ -164,7 +171,7 @@ def tile_mappedattention_pa_t_kernel(tc, head, tail, v1, g1, b1, out_0, out_1, o
             st_hp[(i, a)] = hp
 
         def h_evac(i, a, eng):
-            if a == 0:
+            if i not in st_ho:
                 ho_new = hop.tile([P, 4, D], F32, name="ho", tag="ho")
                 st_ho[i] = ho_new
             ho = st_ho[i]
@@ -173,8 +180,13 @@ def tile_mappedattention_pa_t_kernel(tc, head, tail, v1, g1, b1, out_0, out_1, o
                 ho[:, a, :].rearrange("q (p t) -> q p t", t=4),
                 st_hp[(i, a)][:].rearrange("q t p -> q p t"),
             )
-            if a % 2 == 1:
-                st = a // 2
+            st = a // 2
+            if i == B - 1:
+                nc.sync.dma_start(
+                    out=h_outs[st][i].rearrange("(q j) o -> q j o", j=2)[:, a % 2, :],
+                    in_=ho[:, a, :],
+                )
+            elif a % 2 == 1:
                 nc.sync.dma_start(
                     out=h_outs[st][i].rearrange("(q j) o -> q j o", j=2),
                     in_=ho[:, 2 * st:2 * st + 2, :],
@@ -182,7 +194,10 @@ def tile_mappedattention_pa_t_kernel(tc, head, tail, v1, g1, b1, out_0, out_1, o
 
         def a_pe(i, m):
             hc, hs = st_hc[i]
-            if m == 0:
+            if m == 0 and i == B - 1:
+                a_new = psum.tile([P, 2, 2 * P], F32, name="a_ps2", tag="ring")
+                st_a[i] = a_new
+            elif m == 0:
                 a_new = psa.tile([P, 2, 2 * P], F32, name="a_ps", tag="a_ps")
                 st_a[i] = a_new
             nc.tensor.matmul_mx(
@@ -197,120 +212,145 @@ def tile_mappedattention_pa_t_kernel(tc, head, tail, v1, g1, b1, out_0, out_1, o
 
         def a_evac(i):
             at = atp.tile([P, 2, 2 * P], F32, name="at", tag="at")
-            o = at[:].rearrange("p m (q j) -> p m q j", j=2)
-            s = st_a[i][:].rearrange("p m (j q) -> p m q j", j=2)
-            if A_ENG == "v":
-                nc.vector.tensor_scalar(out=o, in0=s, scalar1=inv_sqrt_d, scalar2=None, op0=ALU.mult)
-            else:
-                nc.scalar.activation(out=o, in_=s, func=ACT.Copy, scale=inv_sqrt_d)
+            nc.vector.tensor_scalar(
+                out=at[:].rearrange("p m (q j) -> p m q j", j=2),
+                in0=st_a[i][:].rearrange("p m (j q) -> p m q j", j=2),
+                scalar1=inv_sqrt_d, scalar2=None, op0=ALU.mult,
+            )
             nc.sync.dma_start(out=out_0[i].rearrange("(q m) c -> q m c", m=2), in_=at[:])
 
         ss = const.tile([P, 4], F32, name="ss")
+        rn = const.tile([P, 4], F32, name="rn")
+        g_f = const.tile([P, 4], F32, name="g_f")
         junk_s = const.tile([P, D], BF16, name="junk_s")
         junk_v = const.tile([P, D], BF16, name="junk_v")
-        for t in (0, 2):
+        w1b = const.tile([P, 4, D], BF16, name="w1b")
+        wg = const.tile([P, 4 * P, 2], F32, name="wg", align_bytes=64)
+        wc = const.tile([P, 4 * P], U32, name="wc", align_bytes=64)
+        ws = const.tile([P, 4 * P], U8, name="ws", align_bytes=64)
+
+        def norms(pr):
+            t = 2 * pr
             nc.scalar.activation(out=junk_s[:], in_=v_sb[:, t, :], func=ACT.Square, accum_out=ss[:, t:t + 1])
             nc.vector.scalar_tensor_tensor(
                 out=junk_v[:], in0=v_sb[:, t + 1, :], scalar=1.0, in1=v_sb[:, t + 1, :],
                 op0=ALU.mult, op1=ALU.mult, accum_out=ss[:, t + 1:t + 2],
             )
-        rn = const.tile([P, 4], F32, name="rn")
-        nc.gpsimd.tensor_tensor(out=rn[:], in0=ss[:], in1=minus_half[:], op=ALU.pow)
-        sc = const.tile([P, 4], F32, name="sc")
-        nc.gpsimd.tensor_tensor(out=sc[:], in0=rn[:], in1=g_sb[:], op=ALU.mult)
-        x_pe(0, 0)
-        x_pe(0, 1)
-        x_pe(1, 0)
-        x_pe(1, 1)
-        x_evac(0, 0, "v")
-        x_evac(0, 1, "s")
-        x_evac(1, 0, "s")
-        w1b = const.tile([P, 4, D], BF16, name="w1b")
-        for t in range(4):
-            nc.vector.tensor_scalar(
-                out=w1b[:, t, :], in0=v_sb[:, t, :], scalar1=sc[:, t:t + 1], scalar2=None, op0=ALU.mult,
+            nc.gpsimd.tensor_tensor(
+                out=rn[:, t:t + 2], in0=ss[:, t:t + 2], in1=minus_half[:, t:t + 2], op=ALU.pow
             )
-        wg = const.tile([P, 4 * P, 2], F32, name="wg", align_bytes=64)
-        wps = []
-        for pr in range(2):
+
+        def w_scale(t):
+            nc.vector.tensor_scalar(
+                out=w1b[:, t, :], in0=v_sb[:, t, :], scalar1=rn[:, t:t + 1], scalar2=g_f[:, t:t + 1],
+                op0=ALU.mult, op1=ALU.mult,
+            )
+
+        st_w = {}
+
+        def w_pe(pr):
             wp = psum.tile([P, 2, 2, P], F32, name="wp", tag="ring")
             for a in range(2):
                 ww = w1b[:, 2 * pr + a, :].bitcast(F32)
                 for u in range(2):
                     nc.tensor.transpose(out=wp[:, a, u, :], in_=ww[:, u * P:(u + 1) * P], identity=ident_f[:])
-            wps.append(wp)
-        x_quant(0)
-        for pr in range(2):
+            st_w[pr] = wp
+
+        def w_evac(pr, eng):
             evac(
-                "v" if pr == 0 else "s",
+                eng,
                 wg[:, pr * 256:(pr + 1) * 256, :].rearrange("c (a p) u -> c a p u", a=2),
-                wps[pr][:].rearrange("c a u p -> c a p u"),
+                st_w[pr][:].rearrange("c a u p -> c a p u"),
             )
+
+        def w_quant():
+            nc.vector.quantize_mx(
+                out=wc[:].bitcast(FP8X4), scales=ws[:], in_=wg[:].rearrange("c o u -> c (o u)").bitcast(BF16)
+            )
+
+        norms(0)
+        norms(1)
+        nc.vector.tensor_copy(out=g_f[:], in_=g_sb[:])
+        warm_pe(7)
+        x_pe(0, 0)
+        x_pe(0, 1)
+        warm_pe(3)
+        x_evac(0, 0, "v")
+        x_evac(0, 1, "s")
+        w_scale(0)
+        w_scale(1)
+        w_pe(0)
+        w_evac(0, "s")
+        w_scale(2)
+        w_scale(3)
+        x_quant(0)
+        w_pe(1)
+        x_pe(1, 0)
+        x_pe(1, 1)
+        w_evac(1, "v")
+        x_evac(1, 0, "s")
+        w_quant()
         x_evac(1, 1, "s")
-        x_pe(2, 0)
-        x_pe(2, 1)
-        wc = const.tile([P, 4 * P], U32, name="wc", align_bytes=64)
-        ws = const.tile([P, 4 * P], U8, name="ws", align_bytes=64)
-        nc.vector.quantize_mx(
-            out=wc[:].bitcast(FP8X4), scales=ws[:], in_=wg[:].rearrange("c o u -> c (o u)").bitcast(BF16)
-        )
         x_quant(1)
-        x_evac(2, 0, "v")
-        x_evac(2, 1, "s")
-        x_pe(3, 0)
-        x_pe(3, 1)
-        x_quant(2)
+
+        def eng_h(i, a):
+            return HLATE[a] if B - 4 <= i < B - 1 else HE[i % 2][a]
+
+        def x_tiles(i, half):
+            if i < 2:
+                r = 2 + 2 * i + half
+                return ((r, 0, "v"), (r, 1, "s"))
+            if i + LX < B:
+                return ((i + LX, half, "v"),)
+            return ()
 
         for i in range(B):
-            nx = i + LX
-            if nx >= B:
-                he = ("s", "v", "s", "v")
-            elif i % 4 == 0:
-                he = ("s", "s", "s", "v")
-            else:
-                he = ("s", "s", "s", "s")
-            if i - 3 >= 0:
+            if i >= 3:
                 a_evac(i - 3)
             for half in range(2):
-                if i == 0:
-                    x_evac(LX - 1, half, "s")
-                    if half == 1:
-                        x_quant(LX - 1)
-                if nx < B:
-                    x_pe(nx, half)
-                    x_evac(nx, half, "s" if (i == 1 and half == 1) else "v")
-                if i - 2 >= 0:
-                    for a in (2 * half, 2 * half + 1):
-                        h_pe(i - 2, a)
-                    for a in (2 * half, 2 * half + 1):
-                        h_evac(i - 2, a, he[a])
-                if half == 0 and i - 1 >= 0:
+                xs_ = x_tiles(i, half)
+                for (r, st, e) in xs_:
+                    x_pe(r, st)
+                for (r, st, e) in xs_:
+                    x_evac(r, st, e)
+                hs = ()
+                if half == 0 and i >= 2:
+                    hs = ((i - 2, 2), (i - 2, 3))
+                if half == 1 and i >= 1:
+                    hs = ((i - 1, 0), (i - 1, 1))
+                for (b, a) in hs:
+                    h_pe(b, a)
+                for (b, a) in hs:
+                    h_evac(b, a, eng_h(b, a))
+                if half == 0 and i >= 1:
                     regroup(i - 1)
-                if half == 1:
-                    if i - 1 >= 0:
-                        h_quant(i - 1)
-                    if nx < B:
-                        x_quant(nx)
+                if half == 1 and i >= 1:
+                    h_quant(i - 1)
+                if xs_ and (i < 2 or half == 1):
+                    x_quant(xs_[0][0])
                 for t in (2 * half, 2 * half + 1):
                     z_pe(i, t)
                 for t in (2 * half, 2 * half + 1):
                     gelu(i, t)
-                if i - 2 >= 0:
+                if i >= 2:
                     a_pe(i - 2, half)
-        a_evac(B - 3)
-        regroup(B - 1)
+        last = B - 1
+        a_evac(last - 2)
+        regroup(last)
+        for a in (2, 3):
+            h_pe(last - 1, a)
+        for a in (2, 3):
+            h_evac(last - 1, a, "s")
+        h_quant(last)
+        a_pe(last - 1, 0)
+        a_pe(last - 1, 1)
         for a in range(4):
-            h_pe(B - 2, a)
-        for a in range(4):
-            h_evac(B - 2, a, "s")
-        h_quant(B - 1)
-        a_pe(B - 2, 0)
-        a_pe(B - 2, 1)
-        for a in range(4):
-            h_pe(B - 1, a)
-        a_evac(B - 2)
-        a_pe(B - 1, 0)
-        a_pe(B - 1, 1)
-        for a in range(4):
-            h_evac(B - 1, a, ("s", "s", "v", "s")[a])
-        a_evac(B - 1)
+            h_pe(last, a)
+        a_pe(last, 0)
+        a_pe(last, 1)
+        h_evac(last, 0, "s")
+        h_evac(last, 1, "s")
+        a_evac(last - 1)
+        h_evac(last, 2, "v")
+        h_evac(last, 3, "s")
+        a_evac(last)

@@ -18,7 +18,8 @@ P = 128
 B, S, D = 16, 256, 512
 FLOPS = 2 * (2 * B * S) * D * D + 2 * B * S * S * D
 
-HE = (("s", "v", "s", "s"), ("s", "s", "s", "s"))
+HE = (("s", "s", "v", "s"), ("s", "s", "s", "s"))
+GC = 64
 HLATE = ("s", "v", "v", "s")
 LX = 4
 
@@ -148,9 +149,15 @@ def tile_mappedattention_pa_t_kernel(tc, head, tail, v1, g1, b1, out_0, out_1, o
 
         def regroup(i):
             hg = hgp.tile([P, 4 * P, 4], BF16, name="hg", tag="hg", align_bytes=64)
+            vc = 4 * P - GC
+            nc.gpsimd.tensor_scalar(
+                out=hg[:, vc:, :],
+                in0=st_ht[i][:, :, vc:].rearrange("p t c -> p c t"),
+                scalar1=1.0, scalar2=0.0, op0=ALU.mult, op1=ALU.add,
+            )
             nc.vector.tensor_copy(
-                out=hg[:].rearrange("p (c i) t -> p c t i", i=4),
-                in_=st_ht[i][:].rearrange("p t (c i) -> p c t i", i=4),
+                out=hg[:, 0:vc, :].rearrange("p (c i) t -> p c t i", i=4),
+                in_=st_ht[i][:, :, 0:vc].rearrange("p t (c i) -> p c t i", i=4),
             )
             st_hg[i] = hg
 
@@ -332,8 +339,9 @@ def tile_mappedattention_pa_t_kernel(tc, head, tail, v1, g1, b1, out_0, out_1, o
                     z_pe(i, t)
                 for t in (2 * half, 2 * half + 1):
                     gelu(i, t)
-                if i >= 2:
-                    a_pe(i - 2, half)
+                if i >= 2 and half == 1:
+                    a_pe(i - 2, 0)
+                    a_pe(i - 2, 1)
         last = B - 1
         a_evac(last - 2)
         regroup(last)

@@ -18,8 +18,8 @@ P = 128
 B, S, D = 16, 256, 512
 FLOPS = 2 * (2 * B * S) * D * D + 2 * B * S * S * D
 
-HE = (("s", "s", "v", "s"), ("s", "s", "s", "s"))
-GC = 64
+HE = (("s", "s", "v", "s"), ("s", "s", "s", "s"), ("s", "s", "v", "s"), ("s", "s", "v", "s"))
+GC = 128
 HLATE = ("s", "v", "v", "s")
 LX = 4
 
@@ -33,7 +33,7 @@ def tile_mappedattention_pa_t_kernel(tc, head, tail, v1, g1, b1, out_0, out_1, o
     with ExitStack() as ctx:
         const = ctx.enter_context(tc.tile_pool(name="const", bufs=1))
         xin = ctx.enter_context(tc.tile_pool(name="xin", bufs=1))
-        xgp = ctx.enter_context(tc.tile_pool(name="xgp", bufs=3))
+        xgp = ctx.enter_context(tc.tile_pool(name="xgp", bufs=4))
         xcp = ctx.enter_context(tc.tile_pool(name="xcp", bufs=7))
         htp = ctx.enter_context(tc.tile_pool(name="htp", bufs=3))
         hgp = ctx.enter_context(tc.tile_pool(name="hgp", bufs=2))
@@ -277,15 +277,15 @@ def tile_mappedattention_pa_t_kernel(tc, head, tail, v1, g1, b1, out_0, out_1, o
 
         norms(0)
         norms(1)
-        nc.vector.tensor_copy(out=g_f[:], in_=g_sb[:])
+        nc.scalar.copy(out=g_f[:], in_=g_sb[:])
         warm_pe(7)
         x_pe(0, 0)
         x_pe(0, 1)
-        warm_pe(3)
-        x_evac(0, 0, "v")
-        x_evac(0, 1, "s")
+        warm_pe(4)
         w_scale(0)
         w_scale(1)
+        x_evac(0, 0, "v")
+        x_evac(0, 1, "s")
         w_pe(0)
         w_evac(0, "s")
         w_scale(2)
@@ -301,7 +301,7 @@ def tile_mappedattention_pa_t_kernel(tc, head, tail, v1, g1, b1, out_0, out_1, o
         x_quant(1)
 
         def eng_h(i, a):
-            return HLATE[a] if B - 4 <= i < B - 1 else HE[i % 2][a]
+            return HLATE[a] if B - 4 <= i < B - 1 else HE[i % 4][a]
 
         def x_tiles(i, half):
             if i < 2:
@@ -333,8 +333,10 @@ def tile_mappedattention_pa_t_kernel(tc, head, tail, v1, g1, b1, out_0, out_1, o
                     regroup(i - 1)
                 if half == 1 and i >= 1:
                     h_quant(i - 1)
-                if xs_ and (i < 2 or half == 1):
+                if i < 2:
                     x_quant(xs_[0][0])
+                elif half == 0 and 3 <= i <= B - LX:
+                    x_quant(i - 1 + LX)
                 for t in (2 * half, 2 * half + 1):
                     z_pe(i, t)
                 for t in (2 * half, 2 * half + 1):

@@ -20,8 +20,9 @@ FLOPS = 2 * (2 * B * S) * D * D + 2 * B * S * S * D
 
 HE = (("s", "s", "v", "s"), ("s", "s", "s", "s"), ("s", "s", "v", "s"), ("s", "s", "v", "s"))
 GC = 128
+ND = 1
 HLATE = ("s", "v", "v", "s")
-LX = 4
+LX = ND + 2
 
 
 def tile_mappedattention_pa_t_kernel(tc, head, tail, v1, g1, b1, out_0, out_1, out_2):
@@ -34,7 +35,7 @@ def tile_mappedattention_pa_t_kernel(tc, head, tail, v1, g1, b1, out_0, out_1, o
         const = ctx.enter_context(tc.tile_pool(name="const", bufs=1))
         xin = ctx.enter_context(tc.tile_pool(name="xin", bufs=1))
         xgp = ctx.enter_context(tc.tile_pool(name="xgp", bufs=4))
-        xcp = ctx.enter_context(tc.tile_pool(name="xcp", bufs=7))
+        xcp = ctx.enter_context(tc.tile_pool(name="xcp", bufs=LX + 3))
         htp = ctx.enter_context(tc.tile_pool(name="htp", bufs=3))
         hgp = ctx.enter_context(tc.tile_pool(name="hgp", bufs=2))
         hcp = ctx.enter_context(tc.tile_pool(name="hcp", bufs=3))
@@ -149,12 +150,13 @@ def tile_mappedattention_pa_t_kernel(tc, head, tail, v1, g1, b1, out_0, out_1, o
 
         def regroup(i):
             hg = hgp.tile([P, 4 * P, 4], BF16, name="hg", tag="hg", align_bytes=64)
-            vc = 4 * P - GC
-            nc.gpsimd.tensor_scalar(
-                out=hg[:, vc:, :],
-                in0=st_ht[i][:, :, vc:].rearrange("p t c -> p c t"),
-                scalar1=1.0, scalar2=0.0, op0=ALU.mult, op1=ALU.add,
-            )
+            vc = 4 * P - GC if i < B - 1 else 4 * P
+            if vc < 4 * P:
+                nc.gpsimd.tensor_scalar(
+                    out=hg[:, vc:, :],
+                    in0=st_ht[i][:, :, vc:].rearrange("p t c -> p c t"),
+                    scalar1=1.0, scalar2=0.0, op0=ALU.mult, op1=ALU.add,
+                )
             nc.vector.tensor_copy(
                 out=hg[:, 0:vc, :].rearrange("p (c i) t -> p c t i", i=4),
                 in_=st_ht[i][:, :, 0:vc].rearrange("p t (c i) -> p c t i", i=4),
@@ -304,7 +306,7 @@ def tile_mappedattention_pa_t_kernel(tc, head, tail, v1, g1, b1, out_0, out_1, o
             return HLATE[a] if B - 4 <= i < B - 1 else HE[i % 4][a]
 
         def x_tiles(i, half):
-            if i < 2:
+            if i < ND:
                 r = 2 + 2 * i + half
                 return ((r, 0, "v"), (r, 1, "s"))
             if i + LX < B:
@@ -333,9 +335,9 @@ def tile_mappedattention_pa_t_kernel(tc, head, tail, v1, g1, b1, out_0, out_1, o
                     regroup(i - 1)
                 if half == 1 and i >= 1:
                     h_quant(i - 1)
-                if i < 2:
+                if i < ND:
                     x_quant(xs_[0][0])
-                elif half == 0 and 3 <= i <= B - LX:
+                elif half == 0 and ND + 1 <= i <= B - LX:
                     x_quant(i - 1 + LX)
                 for t in (2 * half, 2 * half + 1):
                     z_pe(i, t)
@@ -352,15 +354,17 @@ def tile_mappedattention_pa_t_kernel(tc, head, tail, v1, g1, b1, out_0, out_1, o
         for a in (2, 3):
             h_evac(last - 1, a, "s")
         h_quant(last)
+        h_pe(last, 0)
+        h_pe(last, 1)
         a_pe(last - 1, 0)
         a_pe(last - 1, 1)
-        for a in range(4):
-            h_pe(last, a)
+        h_pe(last, 2)
+        h_pe(last, 3)
         a_pe(last, 0)
         a_pe(last, 1)
         h_evac(last, 0, "s")
         h_evac(last, 1, "s")
         a_evac(last - 1)
-        h_evac(last, 2, "v")
+        h_evac(last, 2, "s")
         h_evac(last, 3, "s")
         a_evac(last)

import math
from contextlib import ExitStack

import concourse.bass as bass
import concourse.mybir as mybir
import concourse.tile as tile
from concourse.masks import make_identity

F32 = mybir.dt.float32
BF16 = mybir.dt.bfloat16
U32 = mybir.dt.uint32
U8 = mybir.dt.uint8
FP8X4 = mybir.dt.float8_e4m3fn_x4
ACT = mybir.ActivationFunctionType
ALU = mybir.AluOpType

P = 128
B, S, D = 16, 256, 512
FLOPS = 2 * (2 * B * S) * D * D + 2 * B * S * S * D

HE = (("s", "s", "v", "s"), ("s", "s", "s", "s"), ("s", "s", "v", "s"), ("s", "s", "v", "s"))
GC = 128
ND = 1
HLATE = ("s", "v", "v", "s")
LX = ND + 2


def tile_mappedattention_pa_t_kernel(tc, head, tail, v1, g1, b1, out_0, out_1, out_2):
    nc = tc.nc
    inv_sqrt_d = 1.0 / math.sqrt(float(D))
    streams = (head, tail)
    h_outs = (out_1, out_2)

    with ExitStack() as ctx:
        const = ctx.enter_context(tc.tile_pool(name="const", bufs=1))
        xin = ctx.enter_context(tc.tile_pool(name="xin", bufs=1))
        xgp = ctx.enter_context(tc.tile_pool(name="xgp", bufs=4))
        xcp = ctx.enter_context(tc.tile_pool(name="xcp", bufs=LX + 3))
        htp = ctx.enter_context(tc.tile_pool(name="htp", bufs=3))
        hgp = ctx.enter_context(tc.tile_pool(name="hgp", bufs=2))
        hcp = ctx.enter_context(tc.tile_pool(name="hcp", bufs=3))
        hop = ctx.enter_context(tc.tile_pool(name="hop", bufs=3))
        atp = ctx.enter_context(tc.tile_pool(name="atp", bufs=3))
        psum = ctx.enter_context(tc.psum_pool(name="psum", bufs=7))
        psa = ctx.enter_context(tc.psum_pool(name="psa", bufs=1))
        ctx.enter_context(tc.manual_schedule())

        def evac(eng, out, in_):
            if eng == "v":
                nc.vector.tensor_copy(out=out, in_=in_)
            else:
                nc.scalar.copy(out=out, in_=in_)

        v_sb = const.tile([P, 4, D], BF16, name="v_sb")
        v_rows = v1.rearrange("(p t) k -> p t k", t=4)
        for t in range(4):
            nc.sync.dma_start(out=v_sb[:, t, :], in_=v_rows[:, t, :])
        g_sb = const.tile([P, 4], BF16, name="g_sb")
        b_sb = const.tile([P, 4], BF16, name="b_sb")
        with nc.allow_non_contiguous_dma(reason="four bf16 values to a partition"):
            nc.sync.dma_start(out=g_sb[:], in_=g1.rearrange("(p t) -> p t", t=4))
            nc.sync.dma_start(out=b_sb[:], in_=b1.rearrange("(p t) -> p t", t=4))
        x_sb = {}
        for b in range(B):
            for st in range(2):
                xt = xin.tile([P, 2 * D], BF16, name="x%d_%d" % (st, b))
                nc.sync.dma_start(out=xt[:], in_=streams[st][b].rearrange("(q j) k -> q (j k)", j=2))
                x_sb[(st, b)] = xt

        warm = const.tile([P, D], BF16, name="warm")
        nc.vector.memset(warm[:], 0.0)

        def warm_pe(n):
            wm = psa.tile([P, 2, 2 * P], F32, name="wm", tag="a_ps")
            for k in range(n):
                nc.tensor.matmul(out=wm[:].rearrange("p m c -> p (m c)"), lhsT=warm[:, 0:P], rhs=warm[:], start=True, stop=True)

        dummy = const.tile([P, 1], F32, name="dummy")
        nc.vector.memset(dummy[:], 1.0)
        dummy2 = const.tile([P, 1], F32, name="dummy2")
        nc.scalar.activation(out=dummy2[:], in_=dummy[:], func=ACT.Gelu_apprx_tanh)
        ident_f = const.tile([P, P], F32, name="ident_f")
        make_identity(nc, ident_f[:])
        minus_half = const.tile([P, 4], F32, name="minus_half")
        nc.gpsimd.memset(minus_half[:], -0.5)

        st_x = {}
        st_xg = {}
        st_xc = {}
        st_z = {}
        st_ht = {}
        st_hg = {}
        st_hc = {}
        st_hp = {}
        st_a = {}
        st_ho = {}

        def x_pe(i, st):
            xp = psum.tile([P, 2, 2, P], F32, name="xp", tag="ring")
            xw = x_sb[(st, i)][:].bitcast(F32)
            for j in range(2):
                for u in range(2):
                    off = j * 256 + u * P
                    nc.tensor.transpose(out=xp[:, j, u, :], in_=xw[:, off:off + P], identity=ident_f[:])
            st_x[(i, st)] = xp

        def x_evac(i, st, eng):
            if st == 0:
                xg_new = xgp.tile([P, 4 * P, 2], F32, name="xg", tag="xg", align_bytes=64)
                st_xg[i] = xg_new
            xg = st_xg[i]
            evac(
                eng,
                xg[:, st * 256:(st + 1) * 256, :].rearrange("p (j q) u -> p j q u", j=2),
                st_x[(i, st)][:].rearrange("p j u q -> p j q u"),
            )

        def x_quant(i):
            xc = xcp.tile([P, 4 * P], U32, name="xc", tag="xc", align_bytes=64)
            xs = xcp.tile([P, 4 * P], U8, name="xs", tag="xs", align_bytes=64)
            nc.vector.quantize_mx(
                out=xc[:].bitcast(FP8X4),
                scales=xs[:],
                in_=st_xg[i][:].rearrange("p c u -> p (c u)").bitcast(BF16),
            )
            st_xc[i] = (xc, xs)

        def z_pe(i, t):
            xc, xs = st_xc[i]
            zp = psum.tile([P, 4 * P], F32, name="zp", tag="ring")
            nc.tensor.matmul_mx(
                out=zp[:],
                lhsT=wc[:, t * P:(t + 1) * P].bitcast(FP8X4),
                lhsT_scale=ws[:, t * P:(t + 1) * P],
                rhs=xc[:].bitcast(FP8X4),
                rhs_scale=xs[:],
                start=True,
                stop=True,
            )
            st_z[(i, t)] = zp

        def gelu(i, t):
            if t == 0:
                ht_new = htp.tile([P, 4, 4 * P], F32, name="ht", tag="ht")
                st_ht[i] = ht_new
            nc.scalar.activation(
                out=st_ht[i][:, t, :], in_=st_z[(i, t)][:], func=ACT.Gelu_apprx_tanh,
                bias=b_sb[:, t:t + 1], scale=1.0,
            )

        def regroup(i):
            hg = hgp.tile([P, 4 * P, 4], BF16, name="hg", tag="hg", align_bytes=64)
            vc = 4 * P - GC if i < B - 1 else 4 * P
            if vc < 4 * P:
                nc.gpsimd.tensor_scalar(
                    out=hg[:, vc:, :],
                    in0=st_ht[i][:, :, vc:].rearrange("p t c -> p c t"),
                    scalar1=1.0, scalar2=0.0, op0=ALU.mult, op1=ALU.add,
                )
            nc.vector.tensor_copy(
                out=hg[:, 0:vc, :].rearrange("p (c i) t -> p c t i", i=4),
                in_=st_ht[i][:, :, 0:vc].rearrange("p t (c i) -> p c t i", i=4),
            )
            st_hg[i] = hg

        def h_quant(i):
            hc = hcp.tile([P, 4 * P], U32, name="hc", tag="hc", align_bytes=64)
            hs = hcp.tile([P, 4 * P], U8, name="hs", tag="hs", align_bytes=64)
            nc.vector.quantize_mx(
                out=hc[:].bitcast(FP8X4),
                scales=hs[:],
                in_=st_hg[i][:].rearrange("p c t -> p (c t)"),
            )
            st_hc[i] = (hc, hs)

        def h_pe(i, a):
            hp = psum.tile([P, 4, P], F32, name="hp", tag="ring")
            for t in range(4):
                nc.tensor.transpose(out=hp[:, t, :], in_=st_ht[i][:, t, a * P:(a + 1) * P], identity=ident_f[:])
            st_hp[(i, a)] = hp

        def h_evac(i, a, eng):
            if i not in st_ho:
                ho_new = hop.tile([P, 4, D], F32, name="ho", tag="ho")
                st_ho[i] = ho_new
            ho = st_ho[i]
            evac(
                eng,
                ho[:, a, :].rearrange("q (p t) -> q p t", t=4),
                st_hp[(i, a)][:].rearrange("q t p -> q p t"),
            )
            st = a // 2
            if i == B - 1:
                nc.sync.dma_start(
                    out=h_outs[st][i].rearrange("(q j) o -> q j o", j=2)[:, a % 2, :],
                    in_=ho[:, a, :],
                )
            elif a % 2 == 1:
                nc.sync.dma_start(
                    out=h_outs[st][i].rearrange("(q j) o -> q j o", j=2),
                    in_=ho[:, 2 * st:2 * st + 2, :],
                )

        def a_pe(i, m):
            hc, hs = st_hc[i]
            if m == 0 and i == B - 1:
                a_new = psum.tile([P, 2, 2 * P], F32, name="a_ps2", tag="ring")
                st_a[i] = a_new
            elif m == 0:
                a_new = psa.tile([P, 2, 2 * P], F32, name="a_ps", tag="a_ps")
                st_a[i] = a_new
            nc.tensor.matmul_mx(
                out=st_a[i][:, m, :],
                lhsT=hc[:, m * P:(m + 1) * P].bitcast(FP8X4),
                lhsT_scale=hs[:, m * P:(m + 1) * P],
                rhs=hc[:, 2 * P:4 * P].bitcast(FP8X4),
                rhs_scale=hs[:, 2 * P:4 * P],
                start=True,
                stop=True,
            )

        def a_evac(i):
            at = atp.tile([P, 2, 2 * P], F32, name="at", tag="at")
            nc.vector.tensor_scalar(
                out=at[:].rearrange("p m (q j) -> p m q j", j=2),
                in0=st_a[i][:].rearrange("p m (j q) -> p m q j", j=2),
                scalar1=inv_sqrt_d, scalar2=None, op0=ALU.mult,
            )
            nc.sync.dma_start(out=out_0[i].rearrange("(q m) c -> q m c", m=2), in_=at[:])

        ss = const.tile([P, 4], F32, name="ss")
        rn = const.tile([P, 4], F32, name="rn")
        g_f = const.tile([P, 4], F32, name="g_f")
        junk_s = const.tile([P, D], BF16, name="junk_s")
        junk_v = const.tile([P, D], BF16, name="junk_v")
        w1b = const.tile([P, 4, D], BF16, name="w1b")
        wg = const.tile([P, 4 * P, 2], F32, name="wg", align_bytes=64)
        wc = const.tile([P, 4 * P], U32, name="wc", align_bytes=64)
        ws = const.tile([P, 4 * P], U8, name="ws", align_bytes=64)

        def norms(pr):
            t = 2 * pr
            nc.scalar.activation(out=junk_s[:], in_=v_sb[:, t, :], func=ACT.Square, accum_out=ss[:, t:t + 1])
            nc.vector.scalar_tensor_tensor(
                out=junk_v[:], in0=v_sb[:, t + 1, :], scalar=1.0, in1=v_sb[:, t + 1, :],
                op0=ALU.mult, op1=ALU.mult, accum_out=ss[:, t + 1:t + 2],
            )
            nc.gpsimd.tensor_tensor(
                out=rn[:, t:t + 2], in0=ss[:, t:t + 2], in1=minus_half[:, t:t + 2], op=ALU.pow
            )

        def w_scale(t):
            nc.vector.tensor_scalar(
                out=w1b[:, t, :], in0=v_sb[:, t, :], scalar1=rn[:, t:t + 1], scalar2=g_f[:, t:t + 1],
                op0=ALU.mult, op1=ALU.mult,
            )

        st_w = {}

        def w_pe(pr):
            wp = psum.tile([P, 2, 2, P], F32, name="wp", tag="ring")
            for a in range(2):
                ww = w1b[:, 2 * pr + a, :].bitcast(F32)
                for u in range(2):
                    nc.tensor.transpose(out=wp[:, a, u, :], in_=ww[:, u * P:(u + 1) * P], identity=ident_f[:])
            st_w[pr] = wp

        def w_evac(pr, eng):
            evac(
                eng,
                wg[:, pr * 256:(pr + 1) * 256, :].rearrange("c (a p) u -> c a p u", a=2),
                st_w[pr][:].rearrange("c a u p -> c a p u"),
            )

        def w_quant():
            nc.vector.quantize_mx(
                out=wc[:].bitcast(FP8X4), scales=ws[:], in_=wg[:].rearrange("c o u -> c (o u)").bitcast(BF16)
            )

        norms(0)
        norms(1)
        nc.scalar.copy(out=g_f[:], in_=g_sb[:])
        warm_pe(7)
        x_pe(0, 0)
        x_pe(0, 1)
        warm_pe(4)
        w_scale(0)
        w_scale(1)
        x_evac(0, 0, "v")
        x_evac(0, 1, "s")
        w_pe(0)
        w_evac(0, "s")
        w_scale(2)
        w_scale(3)
        x_quant(0)
        w_pe(1)
        x_pe(1, 0)
        x_pe(1, 1)
        w_evac(1, "v")
        x_evac(1, 0, "s")
        w_quant()
        x_evac(1, 1, "s")
        x_quant(1)

        def eng_h(i, a):
            return HLATE[a] if B - 4 <= i < B - 1 else HE[i % 4][a]

        def x_tiles(i, half):
            if i < ND:
                r = 2 + 2 * i + half
                return ((r, 0, "v"), (r, 1, "s"))
            if i + LX < B:
                return ((i + LX, half, "v"),)
            return ()

        for i in range(B):
            if i >= 3:
                a_evac(i - 3)
            for half in range(2):
                xs_ = x_tiles(i, half)
                for (r, st, e) in xs_:
                    x_pe(r, st)
                for (r, st, e) in xs_:
                    x_evac(r, st, e)
                hs = ()
                if half == 0 and i >= 2:
                    hs = ((i - 2, 2), (i - 2, 3))
                if half == 1 and i >= 1:
                    hs = ((i - 1, 0), (i - 1, 1))
                for (b, a) in hs:
                    h_pe(b, a)
                for (b, a) in hs:
                    h_evac(b, a, eng_h(b, a))
                if half == 0 and i >= 1:
                    regroup(i - 1)
                if half == 1 and i >= 1:
                    h_quant(i - 1)
                if i < ND:
                    x_quant(xs_[0][0])
                elif half == 0 and ND + 1 <= i <= B - LX:
                    x_quant(i - 1 + LX)
                for t in (2 * half, 2 * half + 1):
                    z_pe(i, t)
                for t in (2 * half, 2 * half + 1):
                    gelu(i, t)
                if i >= 2 and half == 1:
                    a_pe(i - 2, 0)
                    a_pe(i - 2, 1)
        last = B - 1
        a_evac(last - 2)
        regroup(last)
        for a in (2, 3):
            h_pe(last - 1, a)
        for a in (2, 3):
            h_evac(last - 1, a, "s")
        h_quant(last)
        h_pe(last, 0)
        h_pe(last, 1)
        a_pe(last - 1, 0)
        a_pe(last - 1, 1)
        h_pe(last, 2)
        h_pe(last, 3)
        a_pe(last, 0)
        a_pe(last, 1)
        h_evac(last, 0, "s")
        h_evac(last, 1, "s")
        a_evac(last - 1)
        h_evac(last, 2, "s")
        h_evac(last, 3, "s")
        a_evac(last)
